import numpy as np
import ml_dtypes


def mxq(x, axis, fmt="e4m3"):
    dtype, down = {"e4m3": (ml_dtypes.float8_e4m3fn, 7), "e5m2": (ml_dtypes.float8_e5m2, 14)}[fmt]
    v = np.moveaxis(np.asarray(x, np.float32).astype(ml_dtypes.bfloat16).astype(np.float64), axis, -1)
    blocks = v.reshape(v.shape[:-1] + (-1, 32))
    amax = np.abs(blocks).max(-1, keepdims=True)
    byte = np.maximum(np.where(amax > 0, np.frexp(amax)[1] - 1 + 127, 0) - down, 1)
    scale = np.exp2(byte - 127.0)
    codes = (blocks / scale).astype(np.float32).astype(dtype).astype(np.float64)
    return np.moveaxis((codes * scale).reshape(v.shape), -1, axis)


WIDE = False


def mx_kscale(k):
    if not WIDE:
        return np.ones(k)
    levels = np.array([10, -10, 5, -5, 0])
    a = np.random.permutation(np.resize(levels, k // 512 * 4)).reshape(k // 512, 4)
    idx = np.arange(k)
    return np.exp2(a[idx // 512, idx % 128 // 32])


BF16 = ml_dtypes.bfloat16


def bf(x):
    return np.asarray(x, np.float32).astype(BF16)


def f64(x):
    return np.asarray(x).astype(np.float64)


B, L, D, O = 16, 256, 1024, 1


def setup_inputs():
    s, t = mx_kscale(D), mx_kscale(D)
    return {"input1": bf(np.random.standard_normal((B, L, D)) * s),
            "input2": bf(np.random.standard_normal((B, L, D)) / t),
            "w1": bf(np.random.standard_normal((D, O, D)) * (4.0 / D) / s[:, None, None] * t),
            "aff1": bf(np.random.standard_normal((B, L, O))),
            "aff2": bf(np.random.standard_normal((B, L, O))),
            "bias": bf(1.0 + 0.25 * np.random.standard_normal(O))}


def reference(input1, input2, w1, aff1, aff2, bias):
    u = mxq(f64(input1), 2, "e4m3").reshape(B * L, D) @ mxq(f64(w1), 0, "e4m3").reshape(D, O * D)
    u = u.reshape(B, L * O, D)
    p = mxq(u, 2, "e4m3") @ mxq(f64(input2), 2, "e4m3").transpose(0, 2, 1)
    logits_1 = p.reshape(B, L, O, L).transpose(0, 1, 3, 2)
    logits_2 = f64(aff1)[:, :, None, :] + f64(aff2)[:, None, :, :] + f64(bias)
    return logits_1 + logits_2

@@ -1,0 +1,229 @@
+from contextlib import ExitStack
+
+import concourse.mybir as mybir
+from concourse.masks import make_identity
+
+F32 = mybir.dt.float32
+BF16 = mybir.dt.bfloat16
+U32 = mybir.dt.uint32
+U8 = mybir.dt.uint8
+FP8X4 = mybir.dt.float8_e4m3fn_x4
+ADD = mybir.AluOpType.add
+
+B, L, D = 16, 256, 1024
+P = 128
+PACK = 4
+K_PASS = P * PACK
+PASSES = D // K_PASS
+ROW_TILES = L // P
+PAIR = 2
+HALVES = PACK // PAIR
+AHEAD = 4
+
+FLOPS = 2 * B * L * D * D + 2 * B * L * L * D
+
+
+def tile_biaffine_2_pa_t_kernel(tc, input1, input2, w1, aff1, aff2, bias, out):
+    nc = tc.nc
+    with ExitStack() as ctx:
+        const = ctx.enter_context(tc.tile_pool(name="const", bufs=1))
+        w_stage = ctx.enter_context(tc.tile_pool(name="w_stage", bufs=2))
+        raw_pool = ctx.enter_context(tc.tile_pool(name="raw", bufs=AHEAD + 1))
+        grouped_pool = ctx.enter_context(tc.tile_pool(name="grouped", bufs=3))
+        codes_pool = ctx.enter_context(tc.tile_pool(name="codes", bufs=3))
+        result_pool = ctx.enter_context(tc.tile_pool(name="result", bufs=3))
+        psum_t = ctx.enter_context(tc.psum_pool(name="psum_t", bufs=4))
+        psum_u = ctx.enter_context(tc.psum_pool(name="psum_u", bufs=3))
+        psum_o = ctx.enter_context(tc.psum_pool(name="psum_o", bufs=1))
+        ctx.enter_context(tc.manual_schedule())
+
+        def bank_copy(index):
+            return nc.vector.tensor_copy if index % 4 == 3 else nc.scalar.copy
+
+        def load_tokens(tokens, name):
+            raw = raw_pool.tile([P, ROW_TILES, D], BF16, name=name, tag=name)
+            nc.sync.dma_start(out=raw[:], in_=tokens.rearrange("(q r) k -> q r k", r=ROW_TILES))
+            return raw
+
+        in1_raw = {}
+        in2_raw = {}
+
+        def load_round(n):
+            if n + 1 < B:
+                in1_raw[n + 1] = load_tokens(input1[n + 1], "in1_raw")
+            if n < B:
+                in2_raw[n] = load_tokens(input2[n], "in2_raw")
+
+        def load_w_half(g2):
+            w_raw = w_stage.tile([P, PASSES * PACK, K_PASS], BF16, name="w_raw", tag="w_raw")
+            for c in range(PASSES * HALVES):
+                nc.sync.dma_start(
+                    out=w_raw[:, PAIR * c : PAIR * (c + 1), :],
+                    in_=w1[PAIR * P * c : PAIR * P * (c + 1), 0, K_PASS * g2 : K_PASS * (g2 + 1)].rearrange(
+                        "(q e) j -> q e j", e=PAIR
+                    ),
+                )
+            return w_raw
+
+        def transpose_tokens(raw):
+            words = raw[:].bitcast(F32)
+            banks = []
+            for g in range(PASSES):
+                t_bank = psum_t.tile([P, ROW_TILES, HALVES, P], F32, name="t_bank", tag="t_bank")
+                for r in range(ROW_TILES):
+                    for u in range(HALVES):
+                        first = (g * HALVES + u) * P
+                        nc.tensor.transpose(t_bank[:, r, u, :], words[:, r, first : first + P], ident_f32[:])
+                banks.append(t_bank)
+            return banks
+
+        def group_tokens(banks, first_index, name):
+            grouped = grouped_pool.tile([P, PASSES, L * PACK], BF16, name=name, tag=name, align_bytes=64)
+            grouped_words = grouped[:].bitcast(F32)
+            for g in range(PASSES):
+                bank_copy(first_index + g)(
+                    out=grouped_words[:, g, :].rearrange("p (q r u) -> p q r u", r=ROW_TILES, u=HALVES),
+                    in_=banks[g][:].rearrange("p r u q -> p q r u"),
+                )
+            return grouped
+
+        def quantise(grouped_flat, name):
+            codes = codes_pool.tile([P, PASSES, L], U32, name=name + "_codes", tag=name + "_codes", align_bytes=64)
+            scales = codes_pool.tile([P, PASSES, L], U8, name=name + "_scales", tag=name + "_scales", align_bytes=64)
+            nc.vector.quantize_mx(
+                out=codes[:].rearrange("p g c -> p (g c)").bitcast(FP8X4),
+                scales=scales[:].rearrange("p g c -> p (g c)"),
+                in_=grouped_flat,
+            )
+            return codes, scales
+
+        def stage_one(in1_mx):
+            in1_codes, in1_scales = in1_mx
+            u_grouped = grouped_pool.tile([P, PASSES, L, PACK], BF16, name="u_grouped", tag="u_grouped", align_bytes=64)
+            for g2 in range(PASSES):
+                for m in range(ROW_TILES):
+                    x_cols = slice(m * P, (m + 1) * P)
+                    u_bank = psum_u.tile([P, PACK, P], F32, name="u_bank", tag="u_bank")
+                    for t2 in range(PACK):
+                        for g1 in range(PASSES):
+                            nc.tensor.matmul_mx(
+                                out=u_bank[:, t2, :],
+                                lhsT=w_codes[:, g2, t2, g1, :].bitcast(FP8X4),
+                                lhsT_scale=w_scales[:, g2, t2, g1, :],
+                                rhs=in1_codes[:, g1, x_cols].bitcast(FP8X4),
+                                rhs_scale=in1_scales[:, g1, x_cols],
+                                start=(g1 == 0),
+                                stop=(g1 == PASSES - 1),
+                            )
+                    bank_copy(g2 * ROW_TILES + m)(
+                        out=u_grouped[:, g2, x_cols, :], in_=u_bank[:].rearrange("p t x -> p x t")
+                    )
+            return u_grouped
+
+        def stage_two(u_mx, in2_mx):
+            u_codes, u_scales = u_mx
+            in2_codes, in2_scales = in2_mx
+            o_bank = psum_o.tile([P, ROW_TILES, L], F32, name="o_bank", tag="o_bank")
+            for m in range(ROW_TILES):
+                x_cols = slice(m * P, (m + 1) * P)
+                for g2 in range(PASSES):
+                    nc.tensor.matmul_mx(
+                        out=o_bank[:, m, :],
+                        lhsT=u_codes[:, g2, x_cols].bitcast(FP8X4),
+                        lhsT_scale=u_scales[:, g2, x_cols],
+                        rhs=in2_codes[:, g2, :].bitcast(FP8X4),
+                        rhs_scale=in2_scales[:, g2, :],
+                        start=(g2 == 0),
+                        stop=(g2 == PASSES - 1),
+                    )
+            return o_bank
+
+        def finish(b, o_bank):
+            result = result_pool.tile([P, ROW_TILES, L], F32, name="result", tag="result")
+            for m in range(ROW_TILES):
+                nc.vector.scalar_tensor_tensor(
+                    out=result[:, m, :],
+                    in0=o_bank[:, m, :],
+                    scalar=aff1_col[:, b * ROW_TILES + m : b * ROW_TILES + m + 1],
+                    in1=aff2_all[:, b * L : (b + 1) * L],
+                    op0=ADD,
+                    op1=ADD,
+                )
+            nc.sync.dma_start(out=out[b].rearrange("(m p) y o -> p m (y o)", p=P), in_=result[:])
+
+        ident_f32 = const.tile([P, P], F32, name="ident_f32")
+        make_identity(nc, ident_f32[:])
+        ident_bf16 = const.tile([P, P], BF16, name="ident_bf16")
+        make_identity(nc, ident_bf16[:])
+
+        aff_rows = const.tile([P, P], BF16, name="aff_rows")
+        nc.vector.memset(aff_rows[:], 0.0)
+        nc.sync.dma_start(
+            out=aff_rows[0 : B * ROW_TILES, :], in_=aff1.rearrange("b (m p) o -> (b m) (p o)", p=P)
+        )
+        bias_bf16 = const.tile([P, 1], BF16, name="bias_bf16")
+        nc.sync.dma_start(out=bias_bf16[:], in_=bias.partition_broadcast(P))
+
+        in1_raw[0] = load_tokens(input1[0], "in1_raw")
+        w_raw_halves = [load_w_half(g2) for g2 in range(PASSES)]
+        load_round(0)
+        aff2_all = const.tile([P, B * L], BF16, name="aff2_all")
+        nc.sync.dma_start(out=aff2_all[:], in_=aff2.rearrange("b y o -> (b y o)").partition_broadcast(P))
+        for n in range(1, AHEAD):
+            load_round(n)
+
+        aff_bank = psum_o.tile([P, P], BF16, name="aff_bank", tag="o_bank")
+        nc.tensor.transpose(aff_bank[:], aff_rows[:], ident_bf16[:])
+        bias_f32 = const.tile([P, 1], F32, name="bias_f32")
+        nc.vector.tensor_copy(out=bias_f32[:], in_=bias_bf16[:])
+        aff1_col = const.tile([P, B * ROW_TILES], F32, name="aff1_col")
+        nc.vector.tensor_scalar(
+            out=aff1_col[:], in0=aff_bank[:, 0 : B * ROW_TILES], scalar1=bias_f32[:, 0:1], scalar2=None, op0=ADD
+        )
+
+        in1_mx = {}
+        in2_mx = {}
+        u_grouped = {}
+        u_mx = {}
+        o_banks = {}
+
+        in1_grouped = group_tokens(transpose_tokens(in1_raw[0]), 2, "in1_grouped")
+        in1_mx[0] = quantise(in1_grouped[:].rearrange("p g c -> p (g c)"), "in1")
+
+        w_codes = const.tile([P, PASSES, PACK, PASSES, P], U32, name="w_codes", align_bytes=64)
+        w_scales = const.tile([P, PASSES, PACK, PASSES, P], U8, name="w_scales", align_bytes=64)
+        for g2 in range(PASSES):
+            w_grouped = w_stage.tile([P, PACK, PASSES, P, PACK], BF16, name="w_grouped", tag="w_grouped", align_bytes=64)
+            w_sorted = w_raw_halves[g2][:].rearrange(
+                "p (g t) (u q e) -> p u e g q t", g=PASSES, u=HALVES, e=PAIR
+            )
+            for t2 in range(PACK):
+                copy = nc.vector.tensor_copy if t2 % 2 == 0 else nc.scalar.copy
+                copy(out=w_grouped[:, t2], in_=w_sorted[:, t2 // PAIR, t2 % PAIR])
+            for t2 in range(PACK):
+                nc.vector.quantize_mx(
+                    out=w_codes[:, g2, t2].rearrange("p g q -> p (g q)").bitcast(FP8X4),
+                    scales=w_scales[:, g2, t2].rearrange("p g q -> p (g q)"),
+                    in_=w_grouped[:, t2].rearrange("p g q t -> p (g q t)"),
+                )
+
+        for n in range(B + 2):
+            if 1 <= n <= B:
+                u_mx[n - 1] = quantise(u_grouped[n - 1][:].rearrange("p g x t -> p (g x t)"), "u")
+            if n >= 2:
+                finish(n - 2, o_banks[n - 2])
+            load_round(n + AHEAD)
+            if n < B:
+                banks = []
+                if n + 1 < B:
+                    banks = transpose_tokens(in1_raw[n + 1])
+                banks = banks + transpose_tokens(in2_raw[n])
+                if n + 1 < B:
+                    in1_grouped = group_tokens(banks[0:PASSES], 0, "in1_grouped")
+                in2_grouped = group_tokens(banks[-PASSES:], 2, "in2_grouped")
+                if n + 1 < B:
+                    in1_mx[n + 1] = quantise(in1_grouped[:].rearrange("p g c -> p (g c)"), "in1")
+                in2_mx[n] = quantise(in2_grouped[:].rearrange("p g c -> p (g c)"), "in2")
+                u_grouped[n] = stage_one(in1_mx[n])
+            if 1 <= n <= B:
+                o_banks[n - 1] = stage_two(u_mx[n - 1], in2_mx[n - 1])

@@ -19,6 +19,8 @@ ROW_TILES = L // P
 PAIR = 2
 HALVES = PACK // PAIR
 AHEAD = 4
+BANK_F32 = 512
+AFF2_ROWS = B * L // BANK_F32
 
 FLOPS = 2 * B * L * D * D + 2 * B * L * L * D
 
@@ -156,30 +158,48 @@ def tile_biaffine_2_pa_t_kernel(tc, input1, input2, w1, aff1, aff2, bias, out):
         ident_bf16 = const.tile([P, P], BF16, name="ident_bf16")
         make_identity(nc, ident_bf16[:])
 
-        aff_rows = const.tile([P, P], BF16, name="aff_rows")
-        nc.vector.memset(aff_rows[:], 0.0)
+        aff2_rows = const.tile([P, BANK_F32], BF16, name="aff2_rows")
+        nc.vector.memset(aff2_rows[:], 0.0)
         nc.sync.dma_start(
-            out=aff_rows[0 : B * ROW_TILES, :], in_=aff1.rearrange("b (m p) o -> (b m) (p o)", p=P)
+            out=aff2_rows[0:AFF2_ROWS, :], in_=aff2.rearrange("b y o -> (b y o)").rearrange("(c n) -> c n", n=BANK_F32)
+        )
+        aff1_rows = const.tile([P, P], BF16, name="aff1_rows")
+        nc.vector.memset(aff1_rows[:], 0.0)
+        nc.sync.dma_start(
+            out=aff1_rows[0 : B * ROW_TILES, :], in_=aff1.rearrange("b (m p) o -> (b m) (p o)", p=P)
         )
         bias_bf16 = const.tile([P, 1], BF16, name="bias_bf16")
         nc.sync.dma_start(out=bias_bf16[:], in_=bias.partition_broadcast(P))
 
         in1_raw[0] = load_tokens(input1[0], "in1_raw")
         w_raw_halves = [load_w_half(g2) for g2 in range(PASSES)]
-        load_round(0)
-        aff2_all = const.tile([P, B * L], BF16, name="aff2_all")
-        nc.sync.dma_start(out=aff2_all[:], in_=aff2.rearrange("b y o -> (b y o)").partition_broadcast(P))
-        for n in range(1, AHEAD):
+        for n in range(AHEAD):
             load_round(n)
 
         aff_bank = psum_o.tile([P, P], BF16, name="aff_bank", tag="o_bank")
-        nc.tensor.transpose(aff_bank[:], aff_rows[:], ident_bf16[:])
+        nc.tensor.transpose(aff_bank[:], aff1_rows[:], ident_bf16[:])
         bias_f32 = const.tile([P, 1], F32, name="bias_f32")
         nc.vector.tensor_copy(out=bias_f32[:], in_=bias_bf16[:])
         aff1_col = const.tile([P, B * ROW_TILES], F32, name="aff1_col")
         nc.vector.tensor_scalar(
             out=aff1_col[:], in0=aff_bank[:, 0 : B * ROW_TILES], scalar1=bias_f32[:, 0:1], scalar2=None, op0=ADD
         )
+
+        aff2_all = const.tile([P, B * L], BF16, name="aff2_all")
+        for k in range(AFF2_ROWS // 2):
+            spread = psum_t.tile([P, 2, BANK_F32], BF16, name="spread", tag="t_bank")
+            for h in range(2):
+                c = 2 * k + h
+                nc.tensor.matmul(
+                    out=spread[:, h, :],
+                    lhsT=ident_bf16[:, c : c + 1].to_broadcast([P, P]),
+                    rhs=aff2_rows[:],
+                    start=True,
+                    stop=True,
+                )
+            bank_copy(k)(
+                out=aff2_all[:, 2 * BANK_F32 * k : 2 * BANK_F32 * (k + 1)], in_=spread[:].rearrange("p h n -> p (h n)")
+            )
 
         in1_mx = {}
         in2_mx = {}

@@ -18,80 +18,46 @@ PASSES = D // K_PASS
 ROW_TILES = L // P
 PAIR = 2
 HALVES = PACK // PAIR
-AHEAD = 4
-BANK_F32 = 512
-AFF2_ROWS = B * L // BANK_F32
+RUN_TILES = 4
+RAW_TILES = 3 * RUN_TILES
+WORK_BANKS = 7
 
 FLOPS = 2 * B * L * D * D + 2 * B * L * L * D
 
 
 def tile_biaffine_2_pa_t_kernel(tc, input1, input2, w1, aff1, aff2, bias, out):
     nc = tc.nc
+
+    stream = [(input1, "in1", 0), (input1, "in1", 1)]
+    for n in range(1, B, 2):
+        for tokens, name, b in ((input2, "in2", n - 1), (input1, "in1", n + 1), (input2, "in2", n), (input1, "in1", n + 2)):
+            if b < B:
+                stream.append((tokens, name, b))
+
     with ExitStack() as ctx:
         const = ctx.enter_context(tc.tile_pool(name="const", bufs=1))
         w_stage = ctx.enter_context(tc.tile_pool(name="w_stage", bufs=2))
-        raw_pool = ctx.enter_context(tc.tile_pool(name="raw", bufs=AHEAD + 1))
-        grouped_pool = ctx.enter_context(tc.tile_pool(name="grouped", bufs=3))
-        codes_pool = ctx.enter_context(tc.tile_pool(name="codes", bufs=3))
-        result_pool = ctx.enter_context(tc.tile_pool(name="result", bufs=3))
-        psum_t = ctx.enter_context(tc.psum_pool(name="psum_t", bufs=4))
-        psum_u = ctx.enter_context(tc.psum_pool(name="psum_u", bufs=3))
-        psum_o = ctx.enter_context(tc.psum_pool(name="psum_o", bufs=1))
+        raw_pool = ctx.enter_context(tc.tile_pool(name="raw", bufs=RAW_TILES))
+        grouped_pool = ctx.enter_context(tc.tile_pool(name="grouped", bufs=RUN_TILES))
+        codes_pool = ctx.enter_context(tc.tile_pool(name="codes", bufs=RUN_TILES))
+        result_pool = ctx.enter_context(tc.tile_pool(name="result", bufs=4))
+        psum_work = ctx.enter_context(tc.psum_pool(name="psum_work", bufs=WORK_BANKS))
+        psum_out = ctx.enter_context(tc.psum_pool(name="psum_out", bufs=1))
         ctx.enter_context(tc.manual_schedule())
 
-        def bank_copy(index):
-            return nc.vector.tensor_copy if index % 4 == 3 else nc.scalar.copy
+        raw = {}
+        mx = {}
+        out_banks = {}
 
-        def load_tokens(tokens, name):
-            raw = raw_pool.tile([P, ROW_TILES, D], BF16, name=name, tag=name)
-            nc.sync.dma_start(out=raw[:], in_=tokens.rearrange("(q r) k -> q r k", r=ROW_TILES))
-            return raw
+        def load_tokens(k):
+            if k < len(stream):
+                tokens, name, b = stream[k]
+                raw[k] = raw_pool.tile([P, ROW_TILES, D], BF16, name="raw", tag="raw")
+                nc.sync.dma_start(out=raw[k][:], in_=tokens[b].rearrange("(q r) k -> q r k", r=ROW_TILES))
 
-        in1_raw = {}
-        in2_raw = {}
-
-        def load_round(n):
-            if n + 1 < B:
-                in1_raw[n + 1] = load_tokens(input1[n + 1], "in1_raw")
-            if n < B:
-                in2_raw[n] = load_tokens(input2[n], "in2_raw")
-
-        def load_w_half(g2):
-            w_raw = w_stage.tile([P, PASSES * PACK, K_PASS], BF16, name="w_raw", tag="w_raw")
-            for c in range(PASSES * HALVES):
-                nc.sync.dma_start(
-                    out=w_raw[:, PAIR * c : PAIR * (c + 1), :],
-                    in_=w1[PAIR * P * c : PAIR * P * (c + 1), 0, K_PASS * g2 : K_PASS * (g2 + 1)].rearrange(
-                        "(q e) j -> q e j", e=PAIR
-                    ),
-                )
-            return w_raw
-
-        def transpose_tokens(raw):
-            words = raw[:].bitcast(F32)
-            banks = []
-            for g in range(PASSES):
-                t_bank = psum_t.tile([P, ROW_TILES, HALVES, P], F32, name="t_bank", tag="t_bank")
-                for r in range(ROW_TILES):
-                    for u in range(HALVES):
-                        first = (g * HALVES + u) * P
-                        nc.tensor.transpose(t_bank[:, r, u, :], words[:, r, first : first + P], ident_f32[:])
-                banks.append(t_bank)
-            return banks
-
-        def group_tokens(banks, first_index, name):
-            grouped = grouped_pool.tile([P, PASSES, L * PACK], BF16, name=name, tag=name, align_bytes=64)
-            grouped_words = grouped[:].bitcast(F32)
-            for g in range(PASSES):
-                bank_copy(first_index + g)(
-                    out=grouped_words[:, g, :].rearrange("p (q r u) -> p q r u", r=ROW_TILES, u=HALVES),
-                    in_=banks[g][:].rearrange("p r u q -> p q r u"),
-                )
-            return grouped
-
-        def quantise(grouped_flat, name):
-            codes = codes_pool.tile([P, PASSES, L], U32, name=name + "_codes", tag=name + "_codes", align_bytes=64)
-            scales = codes_pool.tile([P, PASSES, L], U8, name=name + "_scales", tag=name + "_scales", align_bytes=64)
+        def quantise(grouped_flat, columns, name):
+            codes = codes_pool.tile([P, PASSES, columns], U32, name=name + "_codes", tag=name + "_codes", align_bytes=64)
+            scales = codes_pool.tile([P, PASSES, columns], U8, name=name + "_scales", tag=name + "_scales", align_bytes=64)
             nc.vector.quantize_mx(
                 out=codes[:].rearrange("p g c -> p (g c)").bitcast(FP8X4),
                 scales=scales[:].rearrange("p g c -> p (g c)"),
@@ -99,124 +65,115 @@ def tile_biaffine_2_pa_t_kernel(tc, input1, input2, w1, aff1, aff2, bias, out):
             )
             return codes, scales
 
-        def stage_one(in1_mx):
-            in1_codes, in1_scales = in1_mx
-            u_grouped = grouped_pool.tile([P, PASSES, L, PACK], BF16, name="u_grouped", tag="u_grouped", align_bytes=64)
+        def token_run(first, count):
+            tiles = range(first, min(first + count, len(stream)))
+            grouped = {}
+            for k in tiles:
+                words = raw[k][:].bitcast(F32)
+                grouped[k] = grouped_pool.tile([P, PASSES, L * PACK], BF16, name="tok_grouped", tag="tok_grouped", align_bytes=64)
+                grouped_words = grouped[k][:].bitcast(F32)
+                for g in range(PASSES):
+                    t_bank = psum_work.tile([P, ROW_TILES, HALVES, P], F32, name="t_bank", tag="bank")
+                    for r in range(ROW_TILES):
+                        for u in range(HALVES):
+                            first_word = (g * HALVES + u) * P
+                            nc.tensor.transpose(t_bank[:, r, u, :], words[:, r, first_word : first_word + P], ident_f32[:])
+                    copy = nc.scalar.copy if g == 0 else nc.vector.tensor_copy
+                    copy(
+                        out=grouped_words[:, g, :].rearrange("p (q r u) -> p q r u", r=ROW_TILES, u=HALVES),
+                        in_=t_bank[:].rearrange("p r u q -> p q r u"),
+                    )
+                load_tokens(k + RAW_TILES)
+            for k in tiles:
+                mx[stream[k][1:]] = quantise(grouped[k][:].rearrange("p g c -> p (g c)"), L, stream[k][1])
+
+        def stage_one(b):
+            in1_codes, in1_scales = mx[("in1", b)]
+            u_grouped = grouped_pool.tile([P, ROW_TILES, PASSES, P, PACK], BF16, name="u_grouped", tag="u_grouped", align_bytes=64)
             for g2 in range(PASSES):
                 for m in range(ROW_TILES):
                     x_cols = slice(m * P, (m + 1) * P)
-                    u_bank = psum_u.tile([P, PACK, P], F32, name="u_bank", tag="u_bank")
-                    for t2 in range(PACK):
+                    u_bank = psum_work.tile([P, PACK, P], F32, name="u_bank", tag="bank")
+                    for t in range(PACK):
                         for g1 in range(PASSES):
                             nc.tensor.matmul_mx(
-                                out=u_bank[:, t2, :],
-                                lhsT=w_codes[:, g2, t2, g1, :].bitcast(FP8X4),
-                                lhsT_scale=w_scales[:, g2, t2, g1, :],
+                                out=u_bank[:, t, :],
+                                lhsT=w_codes[:, g2, t, g1, :].bitcast(FP8X4),
+                                lhsT_scale=w_scales[:, g2, t, g1, :],
                                 rhs=in1_codes[:, g1, x_cols].bitcast(FP8X4),
                                 rhs_scale=in1_scales[:, g1, x_cols],
                                 start=(g1 == 0),
                                 stop=(g1 == PASSES - 1),
                             )
-                    bank_copy(g2 * ROW_TILES + m)(
-                        out=u_grouped[:, g2, x_cols, :], in_=u_bank[:].rearrange("p t x -> p x t")
-                    )
-            return u_grouped
-
-        def stage_two(u_mx, in2_mx):
-            u_codes, u_scales = u_mx
-            in2_codes, in2_scales = in2_mx
-            o_bank = psum_o.tile([P, ROW_TILES, L], F32, name="o_bank", tag="o_bank")
+                    nc.scalar.copy(out=u_grouped[:, m, g2], in_=u_bank[:].rearrange("p t x -> p x t"))
             for m in range(ROW_TILES):
-                x_cols = slice(m * P, (m + 1) * P)
+                mx[("u", b, m)] = quantise(u_grouped[:, m].rearrange("p g x t -> p (g x t)"), P, "u")
+
+        def stage_two(b):
+            in2_codes, in2_scales = mx[("in2", b)]
+            out_banks[b] = psum_out.tile([P, ROW_TILES, L], F32, name="out_bank", tag="out_bank")
+            for m in range(ROW_TILES):
+                u_codes, u_scales = mx[("u", b, m)]
                 for g2 in range(PASSES):
                     nc.tensor.matmul_mx(
-                        out=o_bank[:, m, :],
-                        lhsT=u_codes[:, g2, x_cols].bitcast(FP8X4),
-                        lhsT_scale=u_scales[:, g2, x_cols],
+                        out=out_banks[b][:, m, :],
+                        lhsT=u_codes[:, g2, :].bitcast(FP8X4),
+                        lhsT_scale=u_scales[:, g2, :],
                         rhs=in2_codes[:, g2, :].bitcast(FP8X4),
                         rhs_scale=in2_scales[:, g2, :],
                         start=(g2 == 0),
                         stop=(g2 == PASSES - 1),
                     )
-            return o_bank
 
-        def finish(b, o_bank):
-            result = result_pool.tile([P, ROW_TILES, L], F32, name="result", tag="result")
+        def finish(b):
             for m in range(ROW_TILES):
+                result = result_pool.tile([P, L], F32, name="result", tag="result")
                 nc.vector.scalar_tensor_tensor(
-                    out=result[:, m, :],
-                    in0=o_bank[:, m, :],
-                    scalar=aff1_col[:, b * ROW_TILES + m : b * ROW_TILES + m + 1],
+                    out=result[:],
+                    in0=out_banks[b][:, m, :],
+                    scalar=aff1_bias[:, b * ROW_TILES + m : b * ROW_TILES + m + 1],
                     in1=aff2_all[:, b * L : (b + 1) * L],
                     op0=ADD,
                     op1=ADD,
                 )
-            nc.sync.dma_start(out=out[b].rearrange("(m p) y o -> p m (y o)", p=P), in_=result[:])
+                nc.sync.dma_start(out=out[b, m * P : (m + 1) * P].rearrange("x y o -> x (y o)"), in_=result[:])
 
         ident_f32 = const.tile([P, P], F32, name="ident_f32")
         make_identity(nc, ident_f32[:])
         ident_bf16 = const.tile([P, P], BF16, name="ident_bf16")
         make_identity(nc, ident_bf16[:])
 
-        aff2_rows = const.tile([P, BANK_F32], BF16, name="aff2_rows")
-        nc.vector.memset(aff2_rows[:], 0.0)
-        nc.sync.dma_start(
-            out=aff2_rows[0:AFF2_ROWS, :], in_=aff2.rearrange("b y o -> (b y o)").rearrange("(c n) -> c n", n=BANK_F32)
-        )
         aff1_rows = const.tile([P, P], BF16, name="aff1_rows")
         nc.vector.memset(aff1_rows[:], 0.0)
-        nc.sync.dma_start(
-            out=aff1_rows[0 : B * ROW_TILES, :], in_=aff1.rearrange("b (m p) o -> (b m) (p o)", p=P)
-        )
+        nc.scalar.dma_start(out=aff1_rows[0 : B * ROW_TILES, :], in_=aff1.rearrange("b (m p) o -> (b m) (p o)", p=P))
         bias_bf16 = const.tile([P, 1], BF16, name="bias_bf16")
-        nc.sync.dma_start(out=bias_bf16[:], in_=bias.partition_broadcast(P))
+        nc.scalar.dma_start(out=bias_bf16[:], in_=bias.partition_broadcast(P))
 
-        in1_raw[0] = load_tokens(input1[0], "in1_raw")
-        w_raw_halves = [load_w_half(g2) for g2 in range(PASSES)]
-        for n in range(AHEAD):
-            load_round(n)
-
-        aff_bank = psum_o.tile([P, P], BF16, name="aff_bank", tag="o_bank")
-        nc.tensor.transpose(aff_bank[:], aff1_rows[:], ident_bf16[:])
-        bias_f32 = const.tile([P, 1], F32, name="bias_f32")
-        nc.vector.tensor_copy(out=bias_f32[:], in_=bias_bf16[:])
-        aff1_col = const.tile([P, B * ROW_TILES], F32, name="aff1_col")
-        nc.vector.tensor_scalar(
-            out=aff1_col[:], in0=aff_bank[:, 0 : B * ROW_TILES], scalar1=bias_f32[:, 0:1], scalar2=None, op0=ADD
-        )
-
-        aff2_all = const.tile([P, B * L], BF16, name="aff2_all")
-        for k in range(AFF2_ROWS // 2):
-            spread = psum_t.tile([P, 2, BANK_F32], BF16, name="spread", tag="t_bank")
-            for h in range(2):
-                c = 2 * k + h
-                nc.tensor.matmul(
-                    out=spread[:, h, :],
-                    lhsT=ident_bf16[:, c : c + 1].to_broadcast([P, P]),
-                    rhs=aff2_rows[:],
-                    start=True,
-                    stop=True,
+        load_tokens(0)
+        w_raw = []
+        for g2 in range(PASSES):
+            w_raw.append(w_stage.tile([P, PASSES * PACK, K_PASS], BF16, name="w_raw", tag="w_raw"))
+            for c in range(PASSES * HALVES):
+                nc.sync.dma_start(
+                    out=w_raw[g2][:, PAIR * c : PAIR * (c + 1), :],
+                    in_=w1[PAIR * P * c : PAIR * P * (c + 1), 0, K_PASS * g2 : K_PASS * (g2 + 1)].rearrange(
+                        "(q e) j -> q e j", e=PAIR
+                    ),
                 )
-            bank_copy(k)(
-                out=aff2_all[:, 2 * BANK_F32 * k : 2 * BANK_F32 * (k + 1)], in_=spread[:].rearrange("p h n -> p (h n)")
-            )
+        for k in range(1, 2 + RUN_TILES):
+            load_tokens(k)
+        aff2_all = const.tile([P, B * L], BF16, name="aff2_all")
+        nc.sync.dma_start(out=aff2_all[:], in_=aff2.rearrange("b y o -> (b y o)").partition_broadcast(P))
+        for k in range(2 + RUN_TILES, RAW_TILES):
+            load_tokens(k)
 
-        in1_mx = {}
-        in2_mx = {}
-        u_grouped = {}
-        u_mx = {}
-        o_banks = {}
-
-        in1_grouped = group_tokens(transpose_tokens(in1_raw[0]), 2, "in1_grouped")
-        in1_mx[0] = quantise(in1_grouped[:].rearrange("p g c -> p (g c)"), "in1")
+        token_run(0, 1)
 
         w_codes = const.tile([P, PASSES, PACK, PASSES, P], U32, name="w_codes", align_bytes=64)
         w_scales = const.tile([P, PASSES, PACK, PASSES, P], U8, name="w_scales", align_bytes=64)
         for g2 in range(PASSES):
             w_grouped = w_stage.tile([P, PACK, PASSES, P, PACK], BF16, name="w_grouped", tag="w_grouped", align_bytes=64)
-            w_sorted = w_raw_halves[g2][:].rearrange(
-                "p (g t) (u q e) -> p u e g q t", g=PASSES, u=HALVES, e=PAIR
-            )
+            w_sorted = w_raw[g2][:].rearrange("p (g t) (u q e) -> p u e g q t", g=PASSES, u=HALVES, e=PAIR)
             for t2 in range(PACK):
                 copy = nc.vector.tensor_copy if t2 % 2 == 0 else nc.scalar.copy
                 copy(out=w_grouped[:, t2], in_=w_sorted[:, t2 // PAIR, t2 % PAIR])
@@ -227,23 +184,23 @@ def tile_biaffine_2_pa_t_kernel(tc, input1, input2, w1, aff1, aff2, bias, out):
                     in_=w_grouped[:, t2].rearrange("p g q t -> p (g q t)"),
                 )
 
+        token_run(1, 1)
+
+        aff1_bank = psum_work.tile([P, P], BF16, name="aff1_bank", tag="bank")
+        nc.tensor.transpose(aff1_bank[:], aff1_rows[:], ident_bf16[:])
+        bias_f32 = const.tile([P, 1], F32, name="bias_f32")
+        nc.vector.tensor_copy(out=bias_f32[:], in_=bias_bf16[:])
+        aff1_bias = const.tile([P, B * ROW_TILES], F32, name="aff1_bias")
+        nc.vector.tensor_scalar(
+            out=aff1_bias[:], in0=aff1_bank[:, 0 : B * ROW_TILES], scalar1=bias_f32[:, 0:1], scalar2=None, op0=ADD
+        )
+
         for n in range(B + 2):
-            if 1 <= n <= B:
-                u_mx[n - 1] = quantise(u_grouped[n - 1][:].rearrange("p g x t -> p (g x t)"), "u")
             if n >= 2:
-                finish(n - 2, o_banks[n - 2])
-            load_round(n + AHEAD)
+                finish(n - 2)
+            if n % 2 == 1 and n < B:
+                token_run(2 + RUN_TILES * (n // 2), RUN_TILES)
             if n < B:
-                banks = []
-                if n + 1 < B:
-                    banks = transpose_tokens(in1_raw[n + 1])
-                banks = banks + transpose_tokens(in2_raw[n])
-                if n + 1 < B:
-                    in1_grouped = group_tokens(banks[0:PASSES], 0, "in1_grouped")
-                in2_grouped = group_tokens(banks[-PASSES:], 2, "in2_grouped")
-                if n + 1 < B:
-                    in1_mx[n + 1] = quantise(in1_grouped[:].rearrange("p g c -> p (g c)"), "in1")
-                in2_mx[n] = quantise(in2_grouped[:].rearrange("p g c -> p (g c)"), "in2")
-                u_grouped[n] = stage_one(in1_mx[n])
+                stage_one(n)
             if 1 <= n <= B:
-                o_banks[n - 1] = stage_two(u_mx[n - 1], in2_mx[n - 1])
+                stage_two(n - 1)

from contextlib import ExitStack

import concourse.mybir as mybir
from concourse.masks import make_identity

F32 = mybir.dt.float32
BF16 = mybir.dt.bfloat16
U32 = mybir.dt.uint32
U8 = mybir.dt.uint8
FP8X4 = mybir.dt.float8_e4m3fn_x4
ADD = mybir.AluOpType.add

B, L, D = 16, 256, 1024
P = 128
PACK = 4
K_PASS = P * PACK
PASSES = D // K_PASS
ROW_TILES = L // P
PAIR = 2
HALVES = PACK // PAIR
RUN_TILES = 4
RAW_TILES = 3 * RUN_TILES
WORK_BANKS = 7

FLOPS = 2 * B * L * D * D + 2 * B * L * L * D


def tile_biaffine_2_pa_t_kernel(tc, input1, input2, w1, aff1, aff2, bias, out):
    nc = tc.nc

    stream = [(input1, "in1", 0), (input1, "in1", 1)]
    for n in range(1, B, 2):
        for tokens, name, b in ((input2, "in2", n - 1), (input1, "in1", n + 1), (input2, "in2", n), (input1, "in1", n + 2)):
            if b < B:
                stream.append((tokens, name, b))

    with ExitStack() as ctx:
        const = ctx.enter_context(tc.tile_pool(name="const", bufs=1))
        w_stage = ctx.enter_context(tc.tile_pool(name="w_stage", bufs=2))
        raw_pool = ctx.enter_context(tc.tile_pool(name="raw", bufs=RAW_TILES))
        grouped_pool = ctx.enter_context(tc.tile_pool(name="grouped", bufs=RUN_TILES))
        codes_pool = ctx.enter_context(tc.tile_pool(name="codes", bufs=RUN_TILES))
        result_pool = ctx.enter_context(tc.tile_pool(name="result", bufs=4))
        psum_work = ctx.enter_context(tc.psum_pool(name="psum_work", bufs=WORK_BANKS))
        psum_out = ctx.enter_context(tc.psum_pool(name="psum_out", bufs=1))
        ctx.enter_context(tc.manual_schedule())

        raw = {}
        mx = {}
        out_banks = {}

        def load_tokens(k):
            if k < len(stream):
                tokens, name, b = stream[k]
                raw[k] = raw_pool.tile([P, ROW_TILES, D], BF16, name="raw", tag="raw")
                nc.sync.dma_start(out=raw[k][:], in_=tokens[b].rearrange("(q r) k -> q r k", r=ROW_TILES))

        def quantise(grouped_flat, columns, name):
            codes = codes_pool.tile([P, PASSES, columns], U32, name=name + "_codes", tag=name + "_codes", align_bytes=64)
            scales = codes_pool.tile([P, PASSES, columns], U8, name=name + "_scales", tag=name + "_scales", align_bytes=64)
            nc.vector.quantize_mx(
                out=codes[:].rearrange("p g c -> p (g c)").bitcast(FP8X4),
                scales=scales[:].rearrange("p g c -> p (g c)"),
                in_=grouped_flat,
            )
            return codes, scales

        def token_run(first, count):
            tiles = range(first, min(first + count, len(stream)))
            grouped = {}
            for k in tiles:
                words = raw[k][:].bitcast(F32)
                grouped[k] = grouped_pool.tile([P, PASSES, L * PACK], BF16, name="tok_grouped", tag="tok_grouped", align_bytes=64)
                grouped_words = grouped[k][:].bitcast(F32)
                for g in range(PASSES):
                    t_bank = psum_work.tile([P, ROW_TILES, HALVES, P], F32, name="t_bank", tag="bank")
                    for r in range(ROW_TILES):
                        for u in range(HALVES):
                            first_word = (g * HALVES + u) * P
                            nc.tensor.transpose(t_bank[:, r, u, :], words[:, r, first_word : first_word + P], ident_f32[:])
                    copy = nc.scalar.copy if g == 0 else nc.vector.tensor_copy
                    copy(
                        out=grouped_words[:, g, :].rearrange("p (q r u) -> p q r u", r=ROW_TILES, u=HALVES),
                        in_=t_bank[:].rearrange("p r u q -> p q r u"),
                    )
                load_tokens(k + RAW_TILES)
            for k in tiles:
                mx[stream[k][1:]] = quantise(grouped[k][:].rearrange("p g c -> p (g c)"), L, stream[k][1])

        def stage_one(b):
            in1_codes, in1_scales = mx[("in1", b)]
            u_grouped = grouped_pool.tile([P, ROW_TILES, PASSES, P, PACK], BF16, name="u_grouped", tag="u_grouped", align_bytes=64)
            for g2 in range(PASSES):
                for m in range(ROW_TILES):
                    x_cols = slice(m * P, (m + 1) * P)
                    u_bank = psum_work.tile([P, PACK, P], F32, name="u_bank", tag="bank")
                    for t in range(PACK):
                        for g1 in range(PASSES):
                            nc.tensor.matmul_mx(
                                out=u_bank[:, t, :],
                                lhsT=w_codes[:, g2, t, g1, :].bitcast(FP8X4),
                                lhsT_scale=w_scales[:, g2, t, g1, :],
                                rhs=in1_codes[:, g1, x_cols].bitcast(FP8X4),
                                rhs_scale=in1_scales[:, g1, x_cols],
                                start=(g1 == 0),
                                stop=(g1 == PASSES - 1),
                            )
                    nc.scalar.copy(out=u_grouped[:, m, g2], in_=u_bank[:].rearrange("p t x -> p x t"))
            for m in range(ROW_TILES):
                mx[("u", b, m)] = quantise(u_grouped[:, m].rearrange("p g x t -> p (g x t)"), P, "u")

        def stage_two(b):
            in2_codes, in2_scales = mx[("in2", b)]
            out_banks[b] = psum_out.tile([P, ROW_TILES, L], F32, name="out_bank", tag="out_bank")
            for m in range(ROW_TILES):
                u_codes, u_scales = mx[("u", b, m)]
                for g2 in range(PASSES):
                    nc.tensor.matmul_mx(
                        out=out_banks[b][:, m, :],
                        lhsT=u_codes[:, g2, :].bitcast(FP8X4),
                        lhsT_scale=u_scales[:, g2, :],
                        rhs=in2_codes[:, g2, :].bitcast(FP8X4),
                        rhs_scale=in2_scales[:, g2, :],
                        start=(g2 == 0),
                        stop=(g2 == PASSES - 1),
                    )

        def finish(b):
            for m in range(ROW_TILES):
                result = result_pool.tile([P, L], F32, name="result", tag="result")
                nc.vector.scalar_tensor_tensor(
                    out=result[:],
                    in0=out_banks[b][:, m, :],
                    scalar=aff1_bias[:, b * ROW_TILES + m : b * ROW_TILES + m + 1],
                    in1=aff2_all[:, b * L : (b + 1) * L],
                    op0=ADD,
                    op1=ADD,
                )
                nc.sync.dma_start(out=out[b, m * P : (m + 1) * P].rearrange("x y o -> x (y o)"), in_=result[:])

        ident_f32 = const.tile([P, P], F32, name="ident_f32")
        make_identity(nc, ident_f32[:])
        ident_bf16 = const.tile([P, P], BF16, name="ident_bf16")
        make_identity(nc, ident_bf16[:])

        aff1_rows = const.tile([P, P], BF16, name="aff1_rows")
        nc.vector.memset(aff1_rows[:], 0.0)
        nc.scalar.dma_start(out=aff1_rows[0 : B * ROW_TILES, :], in_=aff1.rearrange("b (m p) o -> (b m) (p o)", p=P))
        bias_bf16 = const.tile([P, 1], BF16, name="bias_bf16")
        nc.scalar.dma_start(out=bias_bf16[:], in_=bias.partition_broadcast(P))

        load_tokens(0)
        w_raw = []
        for g2 in range(PASSES):
            w_raw.append(w_stage.tile([P, PASSES * PACK, K_PASS], BF16, name="w_raw", tag="w_raw"))
            for c in range(PASSES * HALVES):
                nc.sync.dma_start(
                    out=w_raw[g2][:, PAIR * c : PAIR * (c + 1), :],
                    in_=w1[PAIR * P * c : PAIR * P * (c + 1), 0, K_PASS * g2 : K_PASS * (g2 + 1)].rearrange(
                        "(q e) j -> q e j", e=PAIR
                    ),
                )
        for k in range(1, 2 + RUN_TILES):
            load_tokens(k)
        aff2_all = const.tile([P, B * L], BF16, name="aff2_all")
        nc.sync.dma_start(out=aff2_all[:], in_=aff2.rearrange("b y o -> (b y o)").partition_broadcast(P))
        for k in range(2 + RUN_TILES, RAW_TILES):
            load_tokens(k)

        token_run(0, 1)

        w_codes = const.tile([P, PASSES, PACK, PASSES, P], U32, name="w_codes", align_bytes=64)
        w_scales = const.tile([P, PASSES, PACK, PASSES, P], U8, name="w_scales", align_bytes=64)
        for g2 in range(PASSES):
            w_grouped = w_stage.tile([P, PACK, PASSES, P, PACK], BF16, name="w_grouped", tag="w_grouped", align_bytes=64)
            w_sorted = w_raw[g2][:].rearrange("p (g t) (u q e) -> p u e g q t", g=PASSES, u=HALVES, e=PAIR)
            for t2 in range(PACK):
                copy = nc.vector.tensor_copy if t2 % 2 == 0 else nc.scalar.copy
                copy(out=w_grouped[:, t2], in_=w_sorted[:, t2 // PAIR, t2 % PAIR])
            for t2 in range(PACK):
                nc.vector.quantize_mx(
                    out=w_codes[:, g2, t2].rearrange("p g q -> p (g q)").bitcast(FP8X4),
                    scales=w_scales[:, g2, t2].rearrange("p g q -> p (g q)"),
                    in_=w_grouped[:, t2].rearrange("p g q t -> p (g q t)"),
                )

        token_run(1, 1)

        aff1_bank = psum_work.tile([P, P], BF16, name="aff1_bank", tag="bank")
        nc.tensor.transpose(aff1_bank[:], aff1_rows[:], ident_bf16[:])
        bias_f32 = const.tile([P, 1], F32, name="bias_f32")
        nc.vector.tensor_copy(out=bias_f32[:], in_=bias_bf16[:])
        aff1_bias = const.tile([P, B * ROW_TILES], F32, name="aff1_bias")
        nc.vector.tensor_scalar(
            out=aff1_bias[:], in0=aff1_bank[:, 0 : B * ROW_TILES], scalar1=bias_f32[:, 0:1], scalar2=None, op0=ADD
        )

        for n in range(B + 2):
            if n >= 2:
                finish(n - 2)
            if n % 2 == 1 and n < B:
                token_run(2 + RUN_TILES * (n // 2), RUN_TILES)
            if n < B:
                stage_one(n)
            if 1 <= n <= B:
                stage_two(n - 1)
